import numpy as np
import ml_dtypes


def mxq(x, axis, fmt="e4m3"):
    dtype, down = {"e4m3": (ml_dtypes.float8_e4m3fn, 7), "e5m2": (ml_dtypes.float8_e5m2, 14)}[fmt]
    v = np.moveaxis(np.asarray(x, np.float32).astype(ml_dtypes.bfloat16).astype(np.float64), axis, -1)
    blocks = v.reshape(v.shape[:-1] + (-1, 32))
    amax = np.abs(blocks).max(-1, keepdims=True)
    byte = np.maximum(np.where(amax > 0, np.frexp(amax)[1] - 1 + 127, 0) - down, 1)
    scale = np.exp2(byte - 127.0)
    codes = (blocks / scale).astype(np.float32).astype(dtype).astype(np.float64)
    return np.moveaxis((codes * scale).reshape(v.shape), -1, axis)


WIDE = False


def mx_kscale(k):
    if not WIDE:
        return np.ones(k)
    levels = np.array([10, -10, 5, -5, 0])
    a = np.random.permutation(np.resize(levels, k // 512 * 4)).reshape(k // 512, 4)
    idx = np.arange(k)
    return np.exp2(a[idx // 512, idx % 128 // 32])


BF16 = ml_dtypes.bfloat16


def bf(x):
    return np.asarray(x, np.float32).astype(BF16)


def f64(x):
    return np.asarray(x).astype(np.float64)


B, S, D, H, HD, M, G = 4, 1024, 512, 4, 128, 512, 3
EPS = 1e-6
HH = H * HD


def silu(v):
    return v / (1.0 + np.exp(-v))


def rmsnorm(x, gain):
    var = np.mean(np.square(x), axis=-1, keepdims=True)
    return x * (1.0 / np.sqrt(var + EPS)) * gain


def setup_inputs():
    s, t = mx_kscale(HH), mx_kscale(D)
    return {"attn": bf(0.3 * np.random.standard_normal((B, S, HH)) * s),
            "x": bf(np.random.standard_normal((B, S, D))),
            "w_o": bf(np.random.standard_normal((HH, D)) * 2.0 / np.sqrt(HH) / s[:, None]),
            "rms2_scale": bf((1.0 + 0.1 * np.random.standard_normal(D)) * t),
            "w_gate": bf(np.random.standard_normal((D, M)) / np.sqrt(D) / t[:, None]),
            "w_up": bf(np.random.standard_normal((D, M)) / np.sqrt(D) / t[:, None])}


def reference(attn, x, w_o, rms2_scale, w_gate, w_up):
    x_mid = f64(x) + (mxq(f64(attn), 2, "e4m3") @ mxq(f64(w_o), 0, "e4m3"))
    hq = mxq(rmsnorm(x_mid, f64(rms2_scale)), 2, "e4m3")
    g = silu(hq @ mxq(f64(w_gate), 0, "e4m3")) * (hq @ mxq(f64(w_up), 0, "e4m3"))
    return x_mid, g

@@ -1,0 +1,255 @@
+from contextlib import ExitStack
+
+import concourse.mybir as mybir
+from concourse.masks import make_identity
+
+F32 = mybir.dt.float32
+BF16 = mybir.dt.bfloat16
+U32 = mybir.dt.uint32
+U8 = mybir.dt.uint8
+FP8X4 = mybir.dt.float8_e4m3fn_x4
+ALU = mybir.AluOpType
+ACT = mybir.ActivationFunctionType
+
+P = 128
+PACK = 4
+HALVES = 2
+D = 512
+TOKENS = 4096
+BLOCK = 2
+BLOCKS = TOKENS // (P * BLOCK)
+CHUNK = 2
+CHUNKS = BLOCKS // CHUNK
+CHUNKS_AHEAD = 3
+EPS = 1e-6
+
+FLOPS = 3 * 2 * TOKENS * D * D
+
+
+def tile_transformerblocktpu_pb_t_kernel(
+    tc, attn, x, w_o, rms2_scale, w_gate, w_up, out_0, out_1
+):
+    nc = tc.nc
+    attn_tiles = attn.flatten_outer_dims().rearrange("(p j) k -> p j k", p=P)
+    x_tiles = x.flatten_outer_dims().rearrange("(p j) k -> p j k", p=P)
+    x_mid_tiles = out_0.flatten_outer_dims().rearrange("(p j) k -> p j k", p=P)
+    g_tiles = out_1.flatten_outer_dims().rearrange("(p j) k -> p j k", p=P)
+
+    with ExitStack() as pools:
+        pools.enter_context(tc.manual_schedule())
+        keep = pools.enter_context(tc.tile_pool(name="keep", bufs=1))
+        stage = pools.enter_context(tc.tile_pool(name="stage", bufs=3))
+        loads = pools.enter_context(tc.tile_pool(name="loads", bufs=CHUNKS))
+        results = pools.enter_context(tc.tile_pool(name="results", bufs=4))
+        work = pools.enter_context(tc.tile_pool(name="work", bufs=3))
+        per_tile = pools.enter_context(tc.tile_pool(name="per_tile", bufs=2 * BLOCK))
+        word_banks = pools.enter_context(tc.psum_pool(name="word_banks", bufs=1))
+        product_banks = pools.enter_context(tc.psum_pool(name="product_banks", bufs=BLOCK))
+
+        attn_in, x_in = {}, {}
+        attn_words, attn_grouped, attn_mx, attn_wo = {}, {}, {}, {}
+        x_mid, sum_sq, inv_rms, h = {}, {}, {}, {}
+        h_words, h_grouped, h_mx, gate_up, silu_gate = {}, {}, {}, {}, {}
+
+        def tiles_of(first_block, blocks):
+            return slice(first_block * BLOCK, (first_block + blocks) * BLOCK)
+
+        def load_chunk(dram_tiles, label, chunk):
+            rows = loads.tile([P, CHUNK, BLOCK, D], BF16, tag=label)
+            nc.sync.dma_start(
+                out=rows[:].rearrange("p c b k -> p (c b) k"), in_=dram_tiles[:, tiles_of(chunk * CHUNK, CHUNK), :]
+            )
+            return rows
+
+        def load_weight(w):
+            raw = stage.tile([P, PACK, D], BF16)
+            nc.sync.dma_start(
+                out=raw[:].rearrange("p (u e) n -> p u e n", u=HALVES),
+                in_=w.rearrange("(u p e) n -> p u e n", u=HALVES, e=2),
+            )
+            return raw
+
+        def regroup_weight(raw, copy):
+            grouped = stage.tile([P, D, PACK], BF16, align_bytes=64)
+            copy(
+                out=grouped[:].rearrange("p (c i) t -> p c t i", i=4),
+                in_=raw[:].rearrange("p t (c i) -> p c t i", i=4),
+            )
+            return grouped
+
+        def quantise_weight(grouped, label):
+            codes = keep.tile([P, D], U32, name=label + "_codes", align_bytes=64)
+            scales = keep.tile([P, D], U8, name=label + "_scales", align_bytes=64)
+            nc.vector.quantize_mx(
+                out=codes[:].bitcast(FP8X4), scales=scales[:], in_=grouped[:].rearrange("p n t -> p (n t)")
+            )
+            return codes, scales
+
+        def transpose(rows, label):
+            words = word_banks.tile([P, BLOCK, HALVES, P], F32, tag=label + "_words")
+            for b in range(BLOCK):
+                row_words = rows[:, b, :].bitcast(F32)
+                for u in range(HALVES):
+                    nc.tensor.transpose(words[:, b, u, :], row_words[:, u * P : (u + 1) * P], identity[:])
+            return words
+
+        def regroup(words, label):
+            grouped = work.tile([P, BLOCK, P, PACK], BF16, tag=label + "_grouped", align_bytes=64)
+            nc.scalar.copy(out=grouped[:].bitcast(F32), in_=words[:].rearrange("p b u r -> p b r u"))
+            return grouped
+
+        def quantise(grouped, label):
+            codes = work.tile([P, BLOCK * P], U32, tag=label + "_codes", align_bytes=64)
+            scales = work.tile([P, BLOCK * P], U8, tag=label + "_scales", align_bytes=64)
+            nc.vector.quantize_mx(
+                out=codes[:].bitcast(FP8X4), scales=scales[:], in_=grouped[:].rearrange("p b r t -> p (b r t)")
+            )
+            return codes, scales
+
+        def product(rows_mx, b, weight_mx, label):
+            bank = product_banks.tile([P, D], F32, tag=label)
+            tokens = slice(b * P, (b + 1) * P)
+            nc.tensor.matmul_mx(
+                out=bank[:],
+                lhsT=rows_mx[0][:, tokens].bitcast(FP8X4),
+                lhsT_scale=rows_mx[1][:, tokens],
+                rhs=weight_mx[0][:].bitcast(FP8X4),
+                rhs_scale=weight_mx[1][:],
+                start=True,
+                stop=True,
+            )
+            return bank
+
+        def transpose_attn(q):
+            attn_words[q] = transpose(attn_in[q // CHUNK][:, q % CHUNK, :, :], "attn")
+
+        def regroup_attn(q):
+            attn_grouped[q] = regroup(attn_words[q], "attn")
+
+        def quantise_attn(q):
+            attn_mx[q] = quantise(attn_grouped[q], "attn")
+
+        def multiply_by_w_o(q):
+            attn_wo[q] = [product(attn_mx[q], b, wo_mx, "attn_wo") for b in range(BLOCK)]
+
+        def add_residual(q):
+            x_mid[q] = results.tile([P, BLOCK, D], F32, name="x_mid")
+            for b in range(BLOCK):
+                nc.vector.tensor_tensor(
+                    out=x_mid[q][:, b, :], in0=attn_wo[q][b][:], in1=x_in[q // CHUNK][:, q % CHUNK, b, :], op=ALU.add
+                )
+            nc.sync.dma_start(out=x_mid_tiles[:, tiles_of(q, 1), :], in_=x_mid[q][:])
+
+        def sum_squares(q):
+            sum_sq[q] = work.tile([P, BLOCK], F32, name="sum_sq")
+            for b in range(BLOCK):
+                squares = per_tile.tile([P, D], BF16)
+                nc.scalar.activation(
+                    out=squares[:], in_=x_mid[q][:, b, :], func=ACT.Square, accum_out=sum_sq[q][:, b : b + 1]
+                )
+
+        def invert_rms(q):
+            mean_sq = work.tile([P, BLOCK], F32)
+            nc.gpsimd.tensor_scalar(
+                out=mean_sq[:], in0=sum_sq[q][:], scalar1=1.0 / D, scalar2=EPS, op0=ALU.mult, op1=ALU.add
+            )
+            inv_rms[q] = work.tile([P, BLOCK], F32, name="inv_rms")
+            nc.gpsimd.tensor_tensor(out=inv_rms[q][:], in0=mean_sq[:], in1=minus_half[:], op=ALU.pow)
+
+        def normalise(q):
+            h[q] = work.tile([P, BLOCK, D], BF16, name="h")
+            for b in range(BLOCK):
+                nc.vector.scalar_tensor_tensor(
+                    out=h[q][:, b, :],
+                    in0=x_mid[q][:, b, :],
+                    scalar=inv_rms[q][:, b : b + 1],
+                    in1=gain[:],
+                    op0=ALU.mult,
+                    op1=ALU.mult,
+                )
+
+        def transpose_h(q):
+            h_words[q] = transpose(h[q], "h")
+
+        def regroup_h(q):
+            h_grouped[q] = regroup(h_words[q], "h")
+
+        def quantise_h(q):
+            h_mx[q] = quantise(h_grouped[q], "h")
+
+        def multiply_by_gate_and_up(q):
+            gate_up[q] = [
+                (product(h_mx[q], b, wg_mx, "gate"), product(h_mx[q], b, wu_mx, "up")) for b in range(BLOCK)
+            ]
+
+        def apply_silu(q):
+            silu_gate[q] = []
+            for b in range(BLOCK):
+                silu_b = per_tile.tile([P, D], F32)
+                nc.scalar.activation(out=silu_b[:], in_=gate_up[q][b][0][:], func=ACT.Silu)
+                silu_gate[q].append(silu_b)
+
+        def multiply_gate_and_up(q):
+            g = results.tile([P, BLOCK, D], F32)
+            for b in range(BLOCK):
+                nc.vector.tensor_tensor(
+                    out=g[:, b, :], in0=gate_up[q][b][1][:], in1=silu_gate[q][b][:], op=ALU.mult
+                )
+            nc.sync.dma_start(out=g_tiles[:, tiles_of(q, 1), :], in_=g[:])
+
+        identity = keep.tile([P, P], F32)
+        make_identity(nc, identity[:])
+        gain_row = keep.tile([P, D], BF16)
+        nc.vector.memset(gain_row[:], 0.0)
+        ones = keep.tile([P, P], BF16)
+        nc.vector.memset(ones[:], 1.0)
+        minus_half = keep.tile([P, BLOCK], F32)
+        nc.vector.memset(minus_half[:], -0.5)
+
+        table_warmer = keep.tile([P, BLOCK], F32)
+        nc.scalar.activation(out=table_warmer[:], in_=minus_half[:], func=ACT.Silu)
+
+        wo_raw = load_weight(w_o)
+        nc.sync.dma_start(out=gain_row[0:1, :], in_=rms2_scale.rearrange("(o n) -> o n", o=1))
+        attn_in[0] = load_chunk(attn_tiles, "attn", 0)
+        x_in[0] = load_chunk(x_tiles, "x", 0)
+        attn_in[1] = load_chunk(attn_tiles, "attn", 1)
+        wg_raw = load_weight(w_gate)
+        wu_raw = load_weight(w_up)
+        x_in[1] = load_chunk(x_tiles, "x", 1)
+
+        gain_bank = product_banks.tile([P, D], F32, tag="attn_wo")
+        nc.tensor.matmul(out=gain_bank[:], lhsT=ones[:], rhs=gain_row[:], start=True, stop=True)
+        gain = keep.tile([P, D], F32)
+        nc.scalar.copy(out=gain[:], in_=gain_bank[:])
+        wo_mx = quantise_weight(regroup_weight(wo_raw, nc.vector.tensor_copy), "wo")
+
+        def at(q, stage_of_block):
+            if 0 <= q < BLOCKS:
+                stage_of_block(q)
+
+        for step in range(-2, BLOCKS + 4):
+            chunk = step // CHUNK + CHUNKS_AHEAD
+            if step % CHUNK == 0 and chunk < CHUNKS:
+                attn_in[chunk] = load_chunk(attn_tiles, "attn", chunk)
+                x_in[chunk] = load_chunk(x_tiles, "x", chunk)
+            at(step - 2, transpose_h)
+            at(step + 2, transpose_attn)
+            at(step + 1, quantise_attn)
+            at(step - 3, quantise_h)
+            at(step - 4, apply_silu)
+            at(step - 2, regroup_h)
+            at(step, add_residual)
+            at(step + 1, multiply_by_w_o)
+            at(step - 4, multiply_gate_and_up)
+            at(step - 3, multiply_by_gate_and_up)
+            at(step, sum_squares)
+            at(step, invert_rms)
+            at(step - 1, normalise)
+            at(step + 2, regroup_attn)
+            if step == 0:
+                wg_grouped = regroup_weight(wg_raw, nc.vector.tensor_copy)
+                wu_grouped = regroup_weight(wu_raw, nc.scalar.copy)
+            if step == 1:
+                wg_mx = quantise_weight(wg_grouped, "wg")
+                wu_mx = quantise_weight(wu_grouped, "wu")

@@ -48,7 +48,7 @@ def tile_transformerblocktpu_pb_t_kernel(
 
         attn_in, x_in = {}, {}
         attn_words, attn_grouped, attn_mx, attn_wo = {}, {}, {}, {}
-        x_mid, sum_sq, inv_rms, h = {}, {}, {}, {}
+        x_mid, x_mid_gain, sum_sq, inv_rms, h = {}, {}, {}, {}, {}
         h_words, h_grouped, h_mx, gate_up, silu_gate = {}, {}, {}, {}, {}
 
         def tiles_of(first_block, blocks):
@@ -156,17 +156,30 @@ def tile_transformerblocktpu_pb_t_kernel(
             inv_rms[q] = work.tile([P, BLOCK], F32, name="inv_rms")
             nc.gpsimd.tensor_tensor(out=inv_rms[q][:], in0=mean_sq[:], in1=minus_half[:], op=ALU.pow)
 
-        def normalise(q):
-            h[q] = work.tile([P, BLOCK, D], BF16, name="h")
-            for b in range(BLOCK):
-                nc.vector.scalar_tensor_tensor(
-                    out=h[q][:, b, :],
-                    in0=x_mid[q][:, b, :],
-                    scalar=inv_rms[q][:, b : b + 1],
-                    in1=gain[:],
-                    op0=ALU.mult,
-                    op1=ALU.mult,
-                )
+        def multiply_by_gain(q):
+            x_mid_gain[q] = work.tile([P, D], F32, name="x_mid_gain")
+            nc.gpsimd.tensor_tensor(out=x_mid_gain[q][:], in0=x_mid[q][:, 1, :], in1=gain[:], op=ALU.mult)
+
+        def normalise_second_tile(q):
+            h[q] = per_tile.tile([P, BLOCK, D], BF16, name="h")
+            nc.gpsimd.tensor_scalar(
+                out=h[q][:, 1, :],
+                in0=x_mid_gain[q][:],
+                scalar1=inv_rms[q][:, 1:2],
+                scalar2=1.0,
+                op0=ALU.mult,
+                op1=ALU.mult,
+            )
+
+        def normalise_first_tile(q):
+            nc.vector.scalar_tensor_tensor(
+                out=h[q][:, 0, :],
+                in0=x_mid[q][:, 0, :],
+                scalar=inv_rms[q][:, 0:1],
+                in1=gain[:],
+                op0=ALU.mult,
+                op1=ALU.mult,
+            )
 
         def transpose_h(q):
             h_words[q] = transpose(h[q], "h")
@@ -240,12 +253,14 @@ def tile_transformerblocktpu_pb_t_kernel(
             at(step - 4, apply_silu)
             at(step - 2, regroup_h)
             at(step, add_residual)
+            at(step, multiply_by_gain)
             at(step + 1, multiply_by_w_o)
             at(step - 4, multiply_gate_and_up)
             at(step - 3, multiply_by_gate_and_up)
             at(step, sum_squares)
             at(step, invert_rms)
-            at(step - 1, normalise)
+            at(step, normalise_second_tile)
+            at(step - 1, normalise_first_tile)
             at(step + 2, regroup_attn)
             if step == 0:
                 wg_grouped = regroup_weight(wg_raw, nc.vector.tensor_copy)

@@ -18,9 +18,6 @@ D = 512
 TOKENS = 4096
 BLOCK = 2
 BLOCKS = TOKENS // (P * BLOCK)
-CHUNK = 2
-CHUNKS = BLOCKS // CHUNK
-CHUNKS_AHEAD = 3
 EPS = 1e-6
 
 FLOPS = 3 * 2 * TOKENS * D * D
@@ -39,27 +36,28 @@ def tile_transformerblocktpu_pb_t_kernel(
         pools.enter_context(tc.manual_schedule())
         keep = pools.enter_context(tc.tile_pool(name="keep", bufs=1))
         stage = pools.enter_context(tc.tile_pool(name="stage", bufs=3))
-        loads = pools.enter_context(tc.tile_pool(name="loads", bufs=CHUNKS))
+        loads = pools.enter_context(tc.tile_pool(name="loads", bufs=BLOCKS))
         results = pools.enter_context(tc.tile_pool(name="results", bufs=4))
         work = pools.enter_context(tc.tile_pool(name="work", bufs=3))
-        per_tile = pools.enter_context(tc.tile_pool(name="per_tile", bufs=2 * BLOCK))
-        word_banks = pools.enter_context(tc.psum_pool(name="word_banks", bufs=1))
-        product_banks = pools.enter_context(tc.psum_pool(name="product_banks", bufs=BLOCK))
+        per_tile = pools.enter_context(tc.tile_pool(name="per_tile", bufs=3 * BLOCK))
+        word_banks = pools.enter_context(tc.psum_pool(name="word_banks", bufs=2))
+        product_banks = pools.enter_context(tc.psum_pool(name="product_banks", bufs=3 * BLOCK))
 
         attn_in, x_in = {}, {}
         attn_words, attn_grouped, attn_mx, attn_wo = {}, {}, {}, {}
-        x_mid, x_mid_gain, sum_sq, inv_rms, h = {}, {}, {}, {}, {}
+        x_mid, sum_sq, inv_rms, h = {}, {}, {}, {}
         h_words, h_grouped, h_mx, gate_up, silu_gate = {}, {}, {}, {}, {}
 
-        def tiles_of(first_block, blocks):
-            return slice(first_block * BLOCK, (first_block + blocks) * BLOCK)
+        def tiles_of(q):
+            return slice(q * BLOCK, (q + 1) * BLOCK)
 
-        def load_chunk(dram_tiles, label, chunk):
-            rows = loads.tile([P, CHUNK, BLOCK, D], BF16, tag=label)
-            nc.sync.dma_start(
-                out=rows[:].rearrange("p c b k -> p (c b) k"), in_=dram_tiles[:, tiles_of(chunk * CHUNK, CHUNK), :]
-            )
-            return rows
+        def load_attn(q):
+            attn_in[q] = loads.tile([P, BLOCK, D], BF16, name="attn_in")
+            nc.sync.dma_start(out=attn_in[q][:], in_=attn_tiles[:, tiles_of(q), :])
+
+        def load_x(q):
+            x_in[q] = loads.tile([P, BLOCK, D], BF16, name="x_in")
+            nc.sync.dma_start(out=x_in[q][:], in_=x_tiles[:, tiles_of(q), :])
 
         def load_weight(w):
             raw = stage.tile([P, PACK, D], BF16)
@@ -85,8 +83,8 @@ def tile_transformerblocktpu_pb_t_kernel(
             )
             return codes, scales
 
-        def transpose(rows, label):
-            words = word_banks.tile([P, BLOCK, HALVES, P], F32, tag=label + "_words")
+        def transpose(rows):
+            words = word_banks.tile([P, BLOCK, HALVES, P], F32)
             for b in range(BLOCK):
                 row_words = rows[:, b, :].bitcast(F32)
                 for u in range(HALVES):
@@ -106,8 +104,8 @@ def tile_transformerblocktpu_pb_t_kernel(
             )
             return codes, scales
 
-        def product(rows_mx, b, weight_mx, label):
-            bank = product_banks.tile([P, D], F32, tag=label)
+        def product(rows_mx, b, weight_mx):
+            bank = product_banks.tile([P, D], F32)
             tokens = slice(b * P, (b + 1) * P)
             nc.tensor.matmul_mx(
                 out=bank[:],
@@ -121,7 +119,7 @@ def tile_transformerblocktpu_pb_t_kernel(
             return bank
 
         def transpose_attn(q):
-            attn_words[q] = transpose(attn_in[q // CHUNK][:, q % CHUNK, :, :], "attn")
+            attn_words[q] = transpose(attn_in[q])
 
         def regroup_attn(q):
             attn_grouped[q] = regroup(attn_words[q], "attn")
@@ -130,15 +128,15 @@ def tile_transformerblocktpu_pb_t_kernel(
             attn_mx[q] = quantise(attn_grouped[q], "attn")
 
         def multiply_by_w_o(q):
-            attn_wo[q] = [product(attn_mx[q], b, wo_mx, "attn_wo") for b in range(BLOCK)]
+            attn_wo[q] = [product(attn_mx[q], b, wo_mx) for b in range(BLOCK)]
 
         def add_residual(q):
             x_mid[q] = results.tile([P, BLOCK, D], F32, name="x_mid")
             for b in range(BLOCK):
                 nc.vector.tensor_tensor(
-                    out=x_mid[q][:, b, :], in0=attn_wo[q][b][:], in1=x_in[q // CHUNK][:, q % CHUNK, b, :], op=ALU.add
+                    out=x_mid[q][:, b, :], in0=attn_wo[q][b][:], in1=x_in[q][:, b, :], op=ALU.add
                 )
-            nc.sync.dma_start(out=x_mid_tiles[:, tiles_of(q, 1), :], in_=x_mid[q][:])
+            nc.sync.dma_start(out=x_mid_tiles[:, tiles_of(q), :], in_=x_mid[q][:])
 
         def sum_squares(q):
             sum_sq[q] = work.tile([P, BLOCK], F32, name="sum_sq")
@@ -156,33 +154,20 @@ def tile_transformerblocktpu_pb_t_kernel(
             inv_rms[q] = work.tile([P, BLOCK], F32, name="inv_rms")
             nc.gpsimd.tensor_tensor(out=inv_rms[q][:], in0=mean_sq[:], in1=minus_half[:], op=ALU.pow)
 
-        def multiply_by_gain(q):
-            x_mid_gain[q] = work.tile([P, D], F32, name="x_mid_gain")
-            nc.gpsimd.tensor_tensor(out=x_mid_gain[q][:], in0=x_mid[q][:, 1, :], in1=gain[:], op=ALU.mult)
-
-        def normalise_second_tile(q):
-            h[q] = per_tile.tile([P, BLOCK, D], BF16, name="h")
-            nc.gpsimd.tensor_scalar(
-                out=h[q][:, 1, :],
-                in0=x_mid_gain[q][:],
-                scalar1=inv_rms[q][:, 1:2],
-                scalar2=1.0,
-                op0=ALU.mult,
-                op1=ALU.mult,
-            )
-
-        def normalise_first_tile(q):
-            nc.vector.scalar_tensor_tensor(
-                out=h[q][:, 0, :],
-                in0=x_mid[q][:, 0, :],
-                scalar=inv_rms[q][:, 0:1],
-                in1=gain[:],
-                op0=ALU.mult,
-                op1=ALU.mult,
-            )
+        def normalise(q):
+            h[q] = work.tile([P, BLOCK, D], BF16, name="h")
+            for b in range(BLOCK):
+                nc.vector.scalar_tensor_tensor(
+                    out=h[q][:, b, :],
+                    in0=x_mid[q][:, b, :],
+                    scalar=inv_rms[q][:, b : b + 1],
+                    in1=gain[:],
+                    op0=ALU.mult,
+                    op1=ALU.mult,
+                )
 
         def transpose_h(q):
-            h_words[q] = transpose(h[q], "h")
+            h_words[q] = transpose(h[q])
 
         def regroup_h(q):
             h_grouped[q] = regroup(h_words[q], "h")
@@ -192,7 +177,7 @@ def tile_transformerblocktpu_pb_t_kernel(
 
         def multiply_by_gate_and_up(q):
             gate_up[q] = [
-                (product(h_mx[q], b, wg_mx, "gate"), product(h_mx[q], b, wu_mx, "up")) for b in range(BLOCK)
+                (product(h_mx[q], b, wg_mx), product(h_mx[q], b, wu_mx)) for b in range(BLOCK)
             ]
 
         def apply_silu(q):
@@ -203,12 +188,10 @@ def tile_transformerblocktpu_pb_t_kernel(
                 silu_gate[q].append(silu_b)
 
         def multiply_gate_and_up(q):
-            g = results.tile([P, BLOCK, D], F32)
             for b in range(BLOCK):
-                nc.vector.tensor_tensor(
-                    out=g[:, b, :], in0=gate_up[q][b][1][:], in1=silu_gate[q][b][:], op=ALU.mult
-                )
-            nc.sync.dma_start(out=g_tiles[:, tiles_of(q, 1), :], in_=g[:])
+                g = per_tile.tile([P, D], F32)
+                nc.vector.tensor_tensor(out=g[:], in0=gate_up[q][b][1][:], in1=silu_gate[q][b][:], op=ALU.mult)
+                nc.sync.dma_start(out=g_tiles[:, q * BLOCK + b, :], in_=g[:])
 
         identity = keep.tile([P, P], F32)
         make_identity(nc, identity[:])
@@ -224,14 +207,17 @@ def tile_transformerblocktpu_pb_t_kernel(
 
         wo_raw = load_weight(w_o)
         nc.sync.dma_start(out=gain_row[0:1, :], in_=rms2_scale.rearrange("(o n) -> o n", o=1))
-        attn_in[0] = load_chunk(attn_tiles, "attn", 0)
-        x_in[0] = load_chunk(x_tiles, "x", 0)
-        attn_in[1] = load_chunk(attn_tiles, "attn", 1)
+        load_attn(0)
+        load_x(0)
+        load_attn(1)
+        load_attn(2)
         wg_raw = load_weight(w_gate)
         wu_raw = load_weight(w_up)
-        x_in[1] = load_chunk(x_tiles, "x", 1)
+        load_x(1)
+        load_attn(3)
+        load_x(2)
 
-        gain_bank = product_banks.tile([P, D], F32, tag="attn_wo")
+        gain_bank = product_banks.tile([P, D], F32, tag="bank")
         nc.tensor.matmul(out=gain_bank[:], lhsT=ones[:], rhs=gain_row[:], start=True, stop=True)
         gain = keep.tile([P, D], F32)
         nc.scalar.copy(out=gain[:], in_=gain_bank[:])
@@ -242,26 +228,22 @@ def tile_transformerblocktpu_pb_t_kernel(
                 stage_of_block(q)
 
         for step in range(-2, BLOCKS + 4):
-            chunk = step // CHUNK + CHUNKS_AHEAD
-            if step % CHUNK == 0 and chunk < CHUNKS:
-                attn_in[chunk] = load_chunk(attn_tiles, "attn", chunk)
-                x_in[chunk] = load_chunk(x_tiles, "x", chunk)
+            at(step + 6, load_attn)
+            at(step + 5, load_x)
             at(step - 2, transpose_h)
             at(step + 2, transpose_attn)
             at(step + 1, quantise_attn)
             at(step - 3, quantise_h)
             at(step - 4, apply_silu)
             at(step - 2, regroup_h)
+            at(step + 2, regroup_attn)
             at(step, add_residual)
-            at(step, multiply_by_gain)
             at(step + 1, multiply_by_w_o)
             at(step - 4, multiply_gate_and_up)
             at(step - 3, multiply_by_gate_and_up)
             at(step, sum_squares)
             at(step, invert_rms)
-            at(step, normalise_second_tile)
-            at(step - 1, normalise_first_tile)
-            at(step + 2, regroup_attn)
+            at(step - 1, normalise)
             if step == 0:
                 wg_grouped = regroup_weight(wg_raw, nc.vector.tensor_copy)
                 wu_grouped = regroup_weight(wu_raw, nc.scalar.copy)

from contextlib import ExitStack

import concourse.mybir as mybir
from concourse.masks import make_identity

F32 = mybir.dt.float32
BF16 = mybir.dt.bfloat16
U32 = mybir.dt.uint32
U8 = mybir.dt.uint8
FP8X4 = mybir.dt.float8_e4m3fn_x4
ALU = mybir.AluOpType
ACT = mybir.ActivationFunctionType

P = 128
PACK = 4
HALVES = 2
D = 512
TOKENS = 4096
BLOCK = 2
BLOCKS = TOKENS // (P * BLOCK)
EPS = 1e-6

FLOPS = 3 * 2 * TOKENS * D * D


def tile_transformerblocktpu_pb_t_kernel(
    tc, attn, x, w_o, rms2_scale, w_gate, w_up, out_0, out_1
):
    nc = tc.nc
    attn_tiles = attn.flatten_outer_dims().rearrange("(p j) k -> p j k", p=P)
    x_tiles = x.flatten_outer_dims().rearrange("(p j) k -> p j k", p=P)
    x_mid_tiles = out_0.flatten_outer_dims().rearrange("(p j) k -> p j k", p=P)
    g_tiles = out_1.flatten_outer_dims().rearrange("(p j) k -> p j k", p=P)

    with ExitStack() as pools:
        pools.enter_context(tc.manual_schedule())
        keep = pools.enter_context(tc.tile_pool(name="keep", bufs=1))
        stage = pools.enter_context(tc.tile_pool(name="stage", bufs=3))
        loads = pools.enter_context(tc.tile_pool(name="loads", bufs=BLOCKS))
        results = pools.enter_context(tc.tile_pool(name="results", bufs=4))
        work = pools.enter_context(tc.tile_pool(name="work", bufs=3))
        per_tile = pools.enter_context(tc.tile_pool(name="per_tile", bufs=3 * BLOCK))
        word_banks = pools.enter_context(tc.psum_pool(name="word_banks", bufs=2))
        product_banks = pools.enter_context(tc.psum_pool(name="product_banks", bufs=3 * BLOCK))

        attn_in, x_in = {}, {}
        attn_words, attn_grouped, attn_mx, attn_wo = {}, {}, {}, {}
        x_mid, sum_sq, inv_rms, h = {}, {}, {}, {}
        h_words, h_grouped, h_mx, gate_up, silu_gate = {}, {}, {}, {}, {}

        def tiles_of(q):
            return slice(q * BLOCK, (q + 1) * BLOCK)

        def load_attn(q):
            attn_in[q] = loads.tile([P, BLOCK, D], BF16, name="attn_in")
            nc.sync.dma_start(out=attn_in[q][:], in_=attn_tiles[:, tiles_of(q), :])

        def load_x(q):
            x_in[q] = loads.tile([P, BLOCK, D], BF16, name="x_in")
            nc.sync.dma_start(out=x_in[q][:], in_=x_tiles[:, tiles_of(q), :])

        def load_weight(w):
            raw = stage.tile([P, PACK, D], BF16)
            nc.sync.dma_start(
                out=raw[:].rearrange("p (u e) n -> p u e n", u=HALVES),
                in_=w.rearrange("(u p e) n -> p u e n", u=HALVES, e=2),
            )
            return raw

        def regroup_weight(raw, copy):
            grouped = stage.tile([P, D, PACK], BF16, align_bytes=64)
            copy(
                out=grouped[:].rearrange("p (c i) t -> p c t i", i=4),
                in_=raw[:].rearrange("p t (c i) -> p c t i", i=4),
            )
            return grouped

        def quantise_weight(grouped, label):
            codes = keep.tile([P, D], U32, name=label + "_codes", align_bytes=64)
            scales = keep.tile([P, D], U8, name=label + "_scales", align_bytes=64)
            nc.vector.quantize_mx(
                out=codes[:].bitcast(FP8X4), scales=scales[:], in_=grouped[:].rearrange("p n t -> p (n t)")
            )
            return codes, scales

        def transpose(rows):
            words = word_banks.tile([P, BLOCK, HALVES, P], F32)
            for b in range(BLOCK):
                row_words = rows[:, b, :].bitcast(F32)
                for u in range(HALVES):
                    nc.tensor.transpose(words[:, b, u, :], row_words[:, u * P : (u + 1) * P], identity[:])
            return words

        def regroup(words, label):
            grouped = work.tile([P, BLOCK, P, PACK], BF16, tag=label + "_grouped", align_bytes=64)
            nc.scalar.copy(out=grouped[:].bitcast(F32), in_=words[:].rearrange("p b u r -> p b r u"))
            return grouped

        def quantise(grouped, label):
            codes = work.tile([P, BLOCK * P], U32, tag=label + "_codes", align_bytes=64)
            scales = work.tile([P, BLOCK * P], U8, tag=label + "_scales", align_bytes=64)
            nc.vector.quantize_mx(
                out=codes[:].bitcast(FP8X4), scales=scales[:], in_=grouped[:].rearrange("p b r t -> p (b r t)")
            )
            return codes, scales

        def product(rows_mx, b, weight_mx):
            bank = product_banks.tile([P, D], F32)
            tokens = slice(b * P, (b + 1) * P)
            nc.tensor.matmul_mx(
                out=bank[:],
                lhsT=rows_mx[0][:, tokens].bitcast(FP8X4),
                lhsT_scale=rows_mx[1][:, tokens],
                rhs=weight_mx[0][:].bitcast(FP8X4),
                rhs_scale=weight_mx[1][:],
                start=True,
                stop=True,
            )
            return bank

        def transpose_attn(q):
            attn_words[q] = transpose(attn_in[q])

        def regroup_attn(q):
            attn_grouped[q] = regroup(attn_words[q], "attn")

        def quantise_attn(q):
            attn_mx[q] = quantise(attn_grouped[q], "attn")

        def multiply_by_w_o(q):
            attn_wo[q] = [product(attn_mx[q], b, wo_mx) for b in range(BLOCK)]

        def add_residual(q):
            x_mid[q] = results.tile([P, BLOCK, D], F32, name="x_mid")
            for b in range(BLOCK):
                nc.vector.tensor_tensor(
                    out=x_mid[q][:, b, :], in0=attn_wo[q][b][:], in1=x_in[q][:, b, :], op=ALU.add
                )
            nc.sync.dma_start(out=x_mid_tiles[:, tiles_of(q), :], in_=x_mid[q][:])

        def sum_squares(q):
            sum_sq[q] = work.tile([P, BLOCK], F32, name="sum_sq")
            for b in range(BLOCK):
                squares = per_tile.tile([P, D], BF16)
                nc.scalar.activation(
                    out=squares[:], in_=x_mid[q][:, b, :], func=ACT.Square, accum_out=sum_sq[q][:, b : b + 1]
                )

        def invert_rms(q):
            mean_sq = work.tile([P, BLOCK], F32)
            nc.gpsimd.tensor_scalar(
                out=mean_sq[:], in0=sum_sq[q][:], scalar1=1.0 / D, scalar2=EPS, op0=ALU.mult, op1=ALU.add
            )
            inv_rms[q] = work.tile([P, BLOCK], F32, name="inv_rms")
            nc.gpsimd.tensor_tensor(out=inv_rms[q][:], in0=mean_sq[:], in1=minus_half[:], op=ALU.pow)

        def normalise(q):
            h[q] = work.tile([P, BLOCK, D], BF16, name="h")
            for b in range(BLOCK):
                nc.vector.scalar_tensor_tensor(
                    out=h[q][:, b, :],
                    in0=x_mid[q][:, b, :],
                    scalar=inv_rms[q][:, b : b + 1],
                    in1=gain[:],
                    op0=ALU.mult,
                    op1=ALU.mult,
                )

        def transpose_h(q):
            h_words[q] = transpose(h[q])

        def regroup_h(q):
            h_grouped[q] = regroup(h_words[q], "h")

        def quantise_h(q):
            h_mx[q] = quantise(h_grouped[q], "h")

        def multiply_by_gate_and_up(q):
            gate_up[q] = [
                (product(h_mx[q], b, wg_mx), product(h_mx[q], b, wu_mx)) for b in range(BLOCK)
            ]

        def apply_silu(q):
            silu_gate[q] = []
            for b in range(BLOCK):
                silu_b = per_tile.tile([P, D], F32)
                nc.scalar.activation(out=silu_b[:], in_=gate_up[q][b][0][:], func=ACT.Silu)
                silu_gate[q].append(silu_b)

        def multiply_gate_and_up(q):
            for b in range(BLOCK):
                g = per_tile.tile([P, D], F32)
                nc.vector.tensor_tensor(out=g[:], in0=gate_up[q][b][1][:], in1=silu_gate[q][b][:], op=ALU.mult)
                nc.sync.dma_start(out=g_tiles[:, q * BLOCK + b, :], in_=g[:])

        identity = keep.tile([P, P], F32)
        make_identity(nc, identity[:])
        gain_row = keep.tile([P, D], BF16)
        nc.vector.memset(gain_row[:], 0.0)
        ones = keep.tile([P, P], BF16)
        nc.vector.memset(ones[:], 1.0)
        minus_half = keep.tile([P, BLOCK], F32)
        nc.vector.memset(minus_half[:], -0.5)

        table_warmer = keep.tile([P, BLOCK], F32)
        nc.scalar.activation(out=table_warmer[:], in_=minus_half[:], func=ACT.Silu)

        wo_raw = load_weight(w_o)
        nc.sync.dma_start(out=gain_row[0:1, :], in_=rms2_scale.rearrange("(o n) -> o n", o=1))
        load_attn(0)
        load_x(0)
        load_attn(1)
        load_attn(2)
        wg_raw = load_weight(w_gate)
        wu_raw = load_weight(w_up)
        load_x(1)
        load_attn(3)
        load_x(2)

        gain_bank = product_banks.tile([P, D], F32, tag="bank")
        nc.tensor.matmul(out=gain_bank[:], lhsT=ones[:], rhs=gain_row[:], start=True, stop=True)
        gain = keep.tile([P, D], F32)
        nc.scalar.copy(out=gain[:], in_=gain_bank[:])
        wo_mx = quantise_weight(regroup_weight(wo_raw, nc.vector.tensor_copy), "wo")

        def at(q, stage_of_block):
            if 0 <= q < BLOCKS:
                stage_of_block(q)

        for step in range(-2, BLOCKS + 4):
            at(step + 6, load_attn)
            at(step + 5, load_x)
            at(step - 2, transpose_h)
            at(step + 2, transpose_attn)
            at(step + 1, quantise_attn)
            at(step - 3, quantise_h)
            at(step - 4, apply_silu)
            at(step - 2, regroup_h)
            at(step + 2, regroup_attn)
            at(step, add_residual)
            at(step + 1, multiply_by_w_o)
            at(step - 4, multiply_gate_and_up)
            at(step - 3, multiply_by_gate_and_up)
            at(step, sum_squares)
            at(step, invert_rms)
            at(step - 1, normalise)
            if step == 0:
                wg_grouped = regroup_weight(wg_raw, nc.vector.tensor_copy)
                wu_grouped = regroup_weight(wu_raw, nc.scalar.copy)
            if step == 1:
                wg_mx = quantise_weight(wg_grouped, "wg")
                wu_mx = quantise_weight(wu_grouped, "wu")
